import numpy as np
import ml_dtypes


def mxq(x, axis, fmt="e4m3"):
    dtype, down = {"e4m3": (ml_dtypes.float8_e4m3fn, 7), "e5m2": (ml_dtypes.float8_e5m2, 14)}[fmt]
    v = np.moveaxis(np.asarray(x, np.float32).astype(ml_dtypes.bfloat16).astype(np.float64), axis, -1)
    blocks = v.reshape(v.shape[:-1] + (-1, 32))
    amax = np.abs(blocks).max(-1, keepdims=True)
    byte = np.maximum(np.where(amax > 0, np.frexp(amax)[1] - 1 + 127, 0) - down, 1)
    scale = np.exp2(byte - 127.0)
    codes = (blocks / scale).astype(np.float32).astype(dtype).astype(np.float64)
    return np.moveaxis((codes * scale).reshape(v.shape), -1, axis)


WIDE = False


def mx_kscale(k):
    if not WIDE:
        return np.ones(k)
    levels = np.array([10, -10, 5, -5, 0])
    a = np.random.permutation(np.resize(levels, k // 512 * 4)).reshape(k // 512, 4)
    idx = np.arange(k)
    return np.exp2(a[idx // 512, idx % 128 // 32])


BF16 = ml_dtypes.bfloat16


def bf(x):
    return np.asarray(x, np.float32).astype(BF16)


def f64(x):
    return np.asarray(x).astype(np.float64)


E2M1 = np.array([0.0, 0.5, 1.0, 1.5, 2.0, 3.0, 4.0, 6.0, -0.0, -0.5, -1.0, -1.5, -2.0, -3.0, -4.0, -6.0])


def pack_weight(w, fmt):
    k, n = w.shape
    w = f64(bf(w)).reshape(k // 32, 32, n)
    amax = np.abs(w).max(1)
    if fmt == "e4m3":
        byte = np.frexp(amax)[1] - 1 + 127 - 7
    else:
        mant, ex = np.frexp(amax / 6.0)
        byte = np.where(mant > 0.5, ex, ex - 1) + 127
    byte = np.clip(np.where(amax > 0, byte, 1), 1, 254)
    scaled = (w * np.exp2(127.0 - byte)[:, None, :]).reshape(k, n).astype(np.float32)
    by_word = np.ascontiguousarray(scaled.reshape(k // 512, 128, 4, n).transpose(0, 1, 3, 2))
    if fmt == "e4m3":
        words = by_word.astype(ml_dtypes.float8_e4m3fn).view(np.uint8)
    else:
        c = by_word.astype(ml_dtypes.float4_e2m1fn).view(np.uint8) & 0xF
        words = c[..., 0::2] | (c[..., 1::2] << 4)
    return np.ascontiguousarray(words), np.ascontiguousarray(byte.astype(np.uint8).reshape(k // 512, 16, n))


def unpack_weight(words, scales, fmt):
    g, p, n, _ = words.shape
    if fmt == "e4m3":
        vals = np.ascontiguousarray(words).view(ml_dtypes.float8_e4m3fn).astype(np.float64)
    else:
        nib = np.empty((g, p, n, 4), np.uint8)
        nib[..., 0::2] = words & 0xF
        nib[..., 1::2] = words >> 4
        vals = E2M1[nib]
    vals = vals * np.repeat(np.exp2(scales.astype(np.float64) - 127.0), 8, axis=1)[..., None]
    return vals.transpose(0, 1, 3, 2).reshape(g * 512, n)


B, T, E, H = 1, 1024, 512, 4
SW = np.sqrt(2.0) * (T / E) ** 0.25 / np.sqrt(E)
FMT = "e4m3"


def setup_inputs():
    s = mx_kscale(E)
    x = bf(np.random.standard_normal((B, T, E)) * s)
    wq = np.random.standard_normal((H, E, E)) * SW / s[:, None]
    wk = np.random.standard_normal((H, E, E)) * SW / s[:, None]
    wq_words, wq_scales = pack_weight(wq.reshape(-1, E), FMT)
    wk_words, wk_scales = pack_weight(wk.reshape(-1, E), FMT)
    return {"x": x,
            "wq_words": wq_words, "wq_scales": wq_scales,
            "wk_words": wk_words, "wk_scales": wk_scales}


def reference(x, wq_words, wq_scales, wk_words, wk_scales):
    xq = mxq(f64(x)[None], 3, "e4m3")
    q = xq @ unpack_weight(wq_words, wq_scales, FMT).reshape(H, E, E)[:, None]
    k = xq @ unpack_weight(wk_words, wk_scales, FMT).reshape(H, E, E)[:, None]
    k_rs = k.reshape(H, B, E, T)
    return (mxq(q, 3, "e4m3") @ mxq(k_rs, 2, "e4m3")) / np.sqrt(T)

@@ -1,0 +1,199 @@
+from contextlib import ExitStack
+
+import concourse.mybir as mybir
+from concourse.masks import make_identity
+
+F32 = mybir.dt.float32
+BF16 = mybir.dt.bfloat16
+I32 = mybir.dt.int32
+U32 = mybir.dt.uint32
+U8 = mybir.dt.uint8
+FP8X4 = mybir.dt.float8_e4m3fn_x4
+
+P = 128
+PACK = 4
+BANK = 512
+HEADS = 4
+TOKENS = 1024
+FEATURES = 512
+TOKEN_TILES = TOKENS // P
+UNITS = HEADS * TOKEN_TILES
+
+Q_AHEAD = 2
+K_AHEAD = TOKEN_TILES + 1
+
+FLOPS = 2 * HEADS * (2 * TOKENS * FEATURES * FEATURES + TOKENS * FEATURES * TOKENS)
+
+
+def tile_multiheadattention_pa_e_kernel(tc, x, wq_words, wq_scales, wk_words, wk_scales, out):
+    nc = tc.nc
+    with ExitStack() as ctx:
+        ctx.enter_context(tc.manual_schedule())
+        const = ctx.enter_context(tc.tile_pool(name="const", bufs=1))
+        key_pool = ctx.enter_context(tc.tile_pool(name="keys", bufs=2))
+        query_pool = ctx.enter_context(tc.tile_pool(name="queries", bufs=4))
+        out_pool = ctx.enter_context(tc.tile_pool(name="scores", bufs=6))
+        psum = ctx.enter_context(tc.psum_pool(name="psum", bufs=8))
+
+        identity = const.tile([P, P], F32)
+        make_identity(nc, identity[:])
+        wq_planes = const.tile([P, FEATURES], U8, align_bytes=64)
+        wk_planes = const.tile([P, FEATURES], U8, align_bytes=64)
+        nc.vector.memset(wk_planes[:].bitcast(I32), 0)
+        nc.vector.memset(wq_planes[:].bitcast(I32), 0)
+        warm = const.tile([P, 1], F32)
+        nc.vector.memset(warm[:], 0.0)
+        nc.scalar.mul(out=warm[:], in_=warm[:], mul=1.0)
+
+        x_rows = const.tile([P, PACK, 2 * FEATURES], BF16)
+        x_view = x[0].rearrange("(c m e) k -> m c (e k)", c=PACK, e=2)
+        for c in range(PACK):
+            nc.sync.dma_start(out=x_rows[:, c, :], in_=x_view[:, c, :])
+        for planes, scales in ((wk_planes, wk_scales), (wq_planes, wq_scales)):
+            for quadrant in range(4):
+                nc.sync.dma_start(
+                    out=planes[32 * quadrant : 32 * quadrant + 4 * HEADS, :].bitcast(I32),
+                    in_=scales[:, 4 * quadrant : 4 * quadrant + 4, :].bitcast(I32),
+                )
+        wq_codes = const.tile([P, HEADS, FEATURES], U32, align_bytes=64)
+        wk_codes = const.tile([P, HEADS, FEATURES], U32, align_bytes=64)
+        for head in range(HEADS):
+            for codes, words in ((wk_codes, wk_words), (wq_codes, wq_words)):
+                nc.sync.dma_start(
+                    out=codes[:, head, :].bitcast(I32),
+                    in_=words[head].rearrange("p n t -> p (n t)").bitcast(I32),
+                )
+
+        x_pairs = x_rows[:].bitcast(F32)
+        x_grouped = const.tile([P, TOKENS * PACK], BF16, align_bytes=64)
+        x_codes = const.tile([P, TOKENS], U32, align_bytes=64)
+        x_scales = const.tile([P, TOKENS], U8, align_bytes=64)
+        pairs = FEATURES // 2
+        for c in range(PACK):
+            x_bank = psum.tile([P, BANK], F32, tag="bank")
+            for e in range(2):
+                for u in range(2):
+                    nc.tensor.transpose(
+                        x_bank[:, (2 * e + u) * P : (2 * e + u + 1) * P],
+                        x_pairs[:, c, pairs * e + u : pairs * (e + 1) : 2],
+                        identity[:],
+                    )
+            nc.scalar.copy(
+                out=x_grouped[:, 2 * P * PACK * c : 2 * P * PACK * (c + 1)]
+                .bitcast(F32)
+                .rearrange("p (e m u) -> p e m u", e=2, u=2),
+                in_=x_bank[:].rearrange("p (e u m) -> p e m u", e=2, u=2),
+            )
+            nc.vector.quantize_mx(
+                out=x_codes[:, 2 * P * c : 2 * P * (c + 1)].bitcast(FP8X4),
+                scales=x_scales[:, 2 * P * c : 2 * P * (c + 1)],
+                in_=x_grouped[:, 2 * P * PACK * c : 2 * P * PACK * (c + 1)],
+            )
+
+        def columns(tile_index):
+            return slice(tile_index * P, (tile_index + 1) * P)
+
+        def regroup(on_scalar, grouped, bank):
+            dst = grouped.rearrange("p (w c) -> p w c", c=PACK)
+            src = bank.rearrange("p (c w) -> p w c", c=PACK)
+            if on_scalar:
+                nc.scalar.copy(out=dst, in_=src)
+            else:
+                nc.vector.tensor_copy(out=dst, in_=src)
+
+        q_grouped = {}
+        q_codes = {}
+        q_scales = {}
+        k_grouped = {}
+        k_codes = {}
+        k_scales = {}
+
+        def project_queries(unit):
+            head, token_tile = divmod(unit, TOKEN_TILES)
+            q_bank = psum.tile([P, BANK], F32, tag="bank")
+            for c in range(PACK):
+                nc.tensor.matmul_mx(
+                    out=q_bank[:, columns(c)],
+                    lhsT=wq_codes[:, head, columns(c)].bitcast(FP8X4),
+                    lhsT_scale=wq_planes[4 * head : P, columns(c)],
+                    rhs=x_codes[:, columns(token_tile)].bitcast(FP8X4),
+                    rhs_scale=x_scales[:, columns(token_tile)],
+                    start=True,
+                    stop=True,
+                )
+            grouped = query_pool.tile([P, P * PACK], BF16, align_bytes=64, tag="q_grouped")
+            regroup(False, grouped[:], q_bank[:])
+            q_grouped[unit] = grouped
+
+        def quantise_queries(unit):
+            codes = query_pool.tile([P, P], U32, align_bytes=64, tag="q_codes")
+            scales = query_pool.tile([P, P], U8, align_bytes=64, tag="q_scales")
+            nc.vector.quantize_mx(out=codes[:].bitcast(FP8X4), scales=scales[:], in_=q_grouped[unit][:])
+            q_codes[unit] = codes
+            q_scales[unit] = scales
+
+        def project_keys(job, on_scalar):
+            head, bank_index = divmod(job, TOKEN_TILES)
+            e, n_tile = divmod(bank_index, PACK)
+            if bank_index == 0:
+                grouped = key_pool.tile([P, TOKENS * PACK], BF16, align_bytes=64, tag="k_grouped")
+                codes = key_pool.tile([P, TOKENS], U32, align_bytes=64, tag="k_codes")
+                scales = key_pool.tile([P, TOKENS], U8, align_bytes=64, tag="k_scales")
+                k_grouped[head] = grouped
+                k_codes[head] = codes
+                k_scales[head] = scales
+            k_bank = psum.tile([P, BANK], F32, tag="bank")
+            for c in range(PACK):
+                nc.tensor.matmul_mx(
+                    out=k_bank[:, columns(c)],
+                    lhsT=x_codes[:, columns(2 * c + e)].bitcast(FP8X4),
+                    lhsT_scale=x_scales[:, columns(2 * c + e)],
+                    rhs=wk_codes[:, head, columns(n_tile)].bitcast(FP8X4),
+                    rhs_scale=wk_planes[4 * head : P, columns(n_tile)],
+                    start=True,
+                    stop=True,
+                )
+            regroup(on_scalar, k_grouped[head][:, BANK * bank_index : BANK * (bank_index + 1)], k_bank[:])
+
+        def quantise_keys(half):
+            head, e = divmod(half, 2)
+            nc.vector.quantize_mx(
+                out=k_codes[head][:, BANK * e : BANK * (e + 1)].bitcast(FP8X4),
+                scales=k_scales[head][:, BANK * e : BANK * (e + 1)],
+                in_=k_grouped[head][:, BANK * PACK * e : BANK * PACK * (e + 1)],
+            )
+
+        def scores(unit):
+            head, token_tile = divmod(unit, TOKEN_TILES)
+            c, e = divmod(token_tile, 2)
+            rows = out_pool.tile([P, TOKENS], F32, tag="rows")
+            for half in range(2):
+                s_bank = psum.tile([P, BANK], F32, tag="bank")
+                nc.tensor.matmul_mx(
+                    out=s_bank[:],
+                    lhsT=q_codes[unit][:].bitcast(FP8X4),
+                    lhsT_scale=q_scales[unit][:],
+                    rhs=k_codes[head][:, BANK * half : BANK * (half + 1)].bitcast(FP8X4),
+                    rhs_scale=k_scales[head][:, BANK * half : BANK * (half + 1)],
+                    start=True,
+                    stop=True,
+                )
+                nc.scalar.mul(out=rows[:, BANK * half : BANK * (half + 1)], in_=s_bank[:], mul=TOKENS**-0.5)
+            nc.sync.dma_start(
+                out=out[head, 0].rearrange("(c m e) j -> c e m j", c=PACK, e=2)[c, e],
+                in_=rows[:],
+            )
+
+        for step in range(-K_AHEAD, UNITS):
+            q_unit = step + Q_AHEAD
+            k_job = step + K_AHEAD
+            if 0 <= q_unit < UNITS:
+                project_queries(q_unit)
+            if k_job < UNITS:
+                project_keys(k_job, k_job % 4 == 3 or (step < 0 and k_job % 2 == 1))
+            if 0 <= q_unit < UNITS:
+                quantise_queries(q_unit)
+            if k_job % 4 == 0 and 0 < k_job <= UNITS:
+                quantise_keys(k_job // 4 - 1)
+            if step >= 0:
+                scores(step)

@@ -20,7 +20,7 @@ TOKEN_TILES = TOKENS // P
 UNITS = HEADS * TOKEN_TILES
 
 Q_AHEAD = 2
-K_AHEAD = TOKEN_TILES + 1
+K_AHEAD = TOKEN_TILES
 
 FLOPS = 2 * HEADS * (2 * TOKENS * FEATURES * FEATURES + TOKENS * FEATURES * TOKENS)
 
@@ -30,8 +30,8 @@ def tile_multiheadattention_pa_e_kernel(tc, x, wq_words, wq_scales, wk_words, wk
     with ExitStack() as ctx:
         ctx.enter_context(tc.manual_schedule())
         const = ctx.enter_context(tc.tile_pool(name="const", bufs=1))
-        key_pool = ctx.enter_context(tc.tile_pool(name="keys", bufs=2))
-        query_pool = ctx.enter_context(tc.tile_pool(name="queries", bufs=4))
+        stage_pool = ctx.enter_context(tc.tile_pool(name="stage", bufs=4))
+        operand_pool = ctx.enter_context(tc.tile_pool(name="operands", bufs=2))
         out_pool = ctx.enter_context(tc.tile_pool(name="scores", bufs=6))
         psum = ctx.enter_context(tc.psum_pool(name="psum", bufs=8))
 
@@ -93,23 +93,35 @@ def tile_multiheadattention_pa_e_kernel(tc, x, wq_words, wq_scales, wk_words, wk
         def columns(tile_index):
             return slice(tile_index * P, (tile_index + 1) * P)
 
-        def regroup(on_scalar, grouped, bank):
-            dst = grouped.rearrange("p (w c) -> p w c", c=PACK)
-            src = bank.rearrange("p (c w) -> p w c", c=PACK)
+        def regroup(bank, on_scalar):
+            grouped = stage_pool.tile([P, BANK], BF16, align_bytes=64, tag="grouped")
+            dst = grouped[:].rearrange("p (w c) -> p w c", c=PACK)
+            src = bank[:].rearrange("p (c w) -> p w c", c=PACK)
             if on_scalar:
                 nc.scalar.copy(out=dst, in_=src)
             else:
                 nc.vector.tensor_copy(out=dst, in_=src)
+            return grouped
 
-        q_grouped = {}
-        q_codes = {}
-        q_scales = {}
-        k_grouped = {}
-        k_codes = {}
-        k_scales = {}
+        def new_operand(name):
+            codes = operand_pool.tile([P, TOKENS], U32, align_bytes=64, tag=name + "_codes", name=name + "_codes")
+            scales = operand_pool.tile([P, TOKENS], U8, align_bytes=64, tag=name + "_scales", name=name + "_scales")
+            return codes, scales
 
-        def project_queries(unit):
-            head, token_tile = divmod(unit, TOKEN_TILES)
+        def quantise(grouped, operand, tile_index):
+            codes, scales = operand
+            nc.vector.quantize_mx(
+                out=codes[:, columns(tile_index)].bitcast(FP8X4),
+                scales=scales[:, columns(tile_index)],
+                in_=grouped[:],
+            )
+
+        queries = {}
+        keys = {}
+
+        def project_queries(head, token_tile, on_scalar):
+            if token_tile == 0:
+                queries[head] = new_operand("q")
             q_bank = psum.tile([P, BANK], F32, tag="bank")
             for c in range(PACK):
                 nc.tensor.matmul_mx(
@@ -121,27 +133,12 @@ def tile_multiheadattention_pa_e_kernel(tc, x, wq_words, wq_scales, wk_words, wk
                     start=True,
                     stop=True,
                 )
-            grouped = query_pool.tile([P, P * PACK], BF16, align_bytes=64, tag="q_grouped")
-            regroup(False, grouped[:], q_bank[:])
-            q_grouped[unit] = grouped
+            return regroup(q_bank, on_scalar)
 
-        def quantise_queries(unit):
-            codes = query_pool.tile([P, P], U32, align_bytes=64, tag="q_codes")
-            scales = query_pool.tile([P, P], U8, align_bytes=64, tag="q_scales")
-            nc.vector.quantize_mx(out=codes[:].bitcast(FP8X4), scales=scales[:], in_=q_grouped[unit][:])
-            q_codes[unit] = codes
-            q_scales[unit] = scales
-
-        def project_keys(job, on_scalar):
-            head, bank_index = divmod(job, TOKEN_TILES)
-            e, n_tile = divmod(bank_index, PACK)
-            if bank_index == 0:
-                grouped = key_pool.tile([P, TOKENS * PACK], BF16, align_bytes=64, tag="k_grouped")
-                codes = key_pool.tile([P, TOKENS], U32, align_bytes=64, tag="k_codes")
-                scales = key_pool.tile([P, TOKENS], U8, align_bytes=64, tag="k_scales")
-                k_grouped[head] = grouped
-                k_codes[head] = codes
-                k_scales[head] = scales
+        def project_keys(head, j_tile, on_scalar):
+            if j_tile == 0:
+                keys[head] = new_operand("k")
+            e, n_tile = divmod(j_tile, PACK)
             k_bank = psum.tile([P, BANK], F32, tag="bank")
             for c in range(PACK):
                 nc.tensor.matmul_mx(
@@ -153,47 +150,45 @@ def tile_multiheadattention_pa_e_kernel(tc, x, wq_words, wq_scales, wk_words, wk
                     start=True,
                     stop=True,
                 )
-            regroup(on_scalar, k_grouped[head][:, BANK * bank_index : BANK * (bank_index + 1)], k_bank[:])
+            return regroup(k_bank, on_scalar)
 
-        def quantise_keys(half):
-            head, e = divmod(half, 2)
-            nc.vector.quantize_mx(
-                out=k_codes[head][:, BANK * e : BANK * (e + 1)].bitcast(FP8X4),
-                scales=k_scales[head][:, BANK * e : BANK * (e + 1)],
-                in_=k_grouped[head][:, BANK * PACK * e : BANK * PACK * (e + 1)],
-            )
-
-        def scores(unit):
-            head, token_tile = divmod(unit, TOKEN_TILES)
-            c, e = divmod(token_tile, 2)
+        def scores(head, token_tile):
+            q_codes, q_scales = queries[head]
+            k_codes, k_scales = keys[head]
             rows = out_pool.tile([P, TOKENS], F32, tag="rows")
             for half in range(2):
+                j_cols = slice(BANK * half, BANK * (half + 1))
                 s_bank = psum.tile([P, BANK], F32, tag="bank")
                 nc.tensor.matmul_mx(
                     out=s_bank[:],
-                    lhsT=q_codes[unit][:].bitcast(FP8X4),
-                    lhsT_scale=q_scales[unit][:],
-                    rhs=k_codes[head][:, BANK * half : BANK * (half + 1)].bitcast(FP8X4),
-                    rhs_scale=k_scales[head][:, BANK * half : BANK * (half + 1)],
+                    lhsT=q_codes[:, columns(token_tile)].bitcast(FP8X4),
+                    lhsT_scale=q_scales[:, columns(token_tile)],
+                    rhs=k_codes[:, j_cols].bitcast(FP8X4),
+                    rhs_scale=k_scales[:, j_cols],
                     start=True,
                     stop=True,
                 )
-                nc.scalar.mul(out=rows[:, BANK * half : BANK * (half + 1)], in_=s_bank[:], mul=TOKENS**-0.5)
+                nc.scalar.mul(out=rows[:, j_cols], in_=s_bank[:], mul=TOKENS**-0.5)
+            c, e = divmod(token_tile, 2)
             nc.sync.dma_start(
                 out=out[head, 0].rearrange("(c m e) j -> c e m j", c=PACK, e=2)[c, e],
                 in_=rows[:],
             )
 
         for step in range(-K_AHEAD, UNITS):
+            k_unit = step + K_AHEAD
             q_unit = step + Q_AHEAD
-            k_job = step + K_AHEAD
-            if 0 <= q_unit < UNITS:
-                project_queries(q_unit)
-            if k_job < UNITS:
-                project_keys(k_job, k_job % 4 == 3 or (step < 0 and k_job % 2 == 1))
-            if 0 <= q_unit < UNITS:
-                quantise_queries(q_unit)
-            if k_job % 4 == 0 and 0 < k_job <= UNITS:
-                quantise_keys(k_job // 4 - 1)
+            project_k = k_unit < UNITS
+            project_q = 0 <= q_unit < UNITS
+            if project_k:
+                k_head, j_tile = divmod(k_unit, TOKEN_TILES)
+                k_grouped = project_keys(k_head, j_tile, j_tile % 4 == 3 or (step < 0 and j_tile % 2 == 1))
+            if project_q:
+                q_head, q_tile = divmod(q_unit, TOKEN_TILES)
+                q_grouped = project_queries(q_head, q_tile, step < 0)
+            if project_k:
+                quantise(k_grouped, keys[k_head], j_tile)
+            if project_q:
+                quantise(q_grouped, queries[q_head], q_tile)
             if step >= 0:
-                scores(step)
+                scores(step // TOKEN_TILES, step % TOKEN_TILES)

@@ -30,9 +30,9 @@ def tile_multiheadattention_pa_e_kernel(tc, x, wq_words, wq_scales, wk_words, wk
     with ExitStack() as ctx:
         ctx.enter_context(tc.manual_schedule())
         const = ctx.enter_context(tc.tile_pool(name="const", bufs=1))
-        stage_pool = ctx.enter_context(tc.tile_pool(name="stage", bufs=4))
+        stage_pool = ctx.enter_context(tc.tile_pool(name="stage", bufs=8))
         operand_pool = ctx.enter_context(tc.tile_pool(name="operands", bufs=2))
-        out_pool = ctx.enter_context(tc.tile_pool(name="scores", bufs=6))
+        out_pool = ctx.enter_context(tc.tile_pool(name="scores", bufs=UNITS))
         psum = ctx.enter_context(tc.psum_pool(name="psum", bufs=8))
 
         identity = const.tile([P, P], F32)
@@ -49,20 +49,29 @@ def tile_multiheadattention_pa_e_kernel(tc, x, wq_words, wq_scales, wk_words, wk
         x_view = x[0].rearrange("(c m e) k -> m c (e k)", c=PACK, e=2)
         for c in range(PACK):
             nc.sync.dma_start(out=x_rows[:, c, :], in_=x_view[:, c, :])
-        for planes, scales in ((wk_planes, wk_scales), (wq_planes, wq_scales)):
+        wq_codes = const.tile([P, HEADS, FEATURES], U32, align_bytes=64)
+        wk_codes = const.tile([P, HEADS, FEATURES], U32, align_bytes=64)
+
+        def load_scales(planes, scales):
             for quadrant in range(4):
                 nc.sync.dma_start(
                     out=planes[32 * quadrant : 32 * quadrant + 4 * HEADS, :].bitcast(I32),
                     in_=scales[:, 4 * quadrant : 4 * quadrant + 4, :].bitcast(I32),
                 )
-        wq_codes = const.tile([P, HEADS, FEATURES], U32, align_bytes=64)
-        wk_codes = const.tile([P, HEADS, FEATURES], U32, align_bytes=64)
-        for head in range(HEADS):
-            for codes, words in ((wk_codes, wk_words), (wq_codes, wq_words)):
-                nc.sync.dma_start(
-                    out=codes[:, head, :].bitcast(I32),
-                    in_=words[head].rearrange("p n t -> p (n t)").bitcast(I32),
-                )
+
+        def load_codes(codes, words, head):
+            nc.sync.dma_start(
+                out=codes[:, head, :].bitcast(I32),
+                in_=words[head].rearrange("p n t -> p (n t)").bitcast(I32),
+            )
+
+        load_scales(wk_planes, wk_scales)
+        load_codes(wk_codes, wk_words, 0)
+        load_scales(wq_planes, wq_scales)
+        load_codes(wq_codes, wq_words, 0)
+        for head in range(1, HEADS):
+            load_codes(wk_codes, wk_words, head)
+            load_codes(wq_codes, wq_words, head)
 
         x_pairs = x_rows[:].bitcast(F32)
         x_grouped = const.tile([P, TOKENS * PACK], BF16, align_bytes=64)

@@ -19,8 +19,7 @@ FEATURES = 512
 TOKEN_TILES = TOKENS // P
 UNITS = HEADS * TOKEN_TILES
 
-Q_AHEAD = 2
-K_AHEAD = TOKEN_TILES
+SLACK = 4
 
 FLOPS = 2 * HEADS * (2 * TOKENS * FEATURES * FEATURES + TOKENS * FEATURES * TOKENS)
 
@@ -45,10 +44,12 @@ def tile_multiheadattention_pa_e_kernel(tc, x, wq_words, wq_scales, wk_words, wk
         nc.vector.memset(warm[:], 0.0)
         nc.scalar.mul(out=warm[:], in_=warm[:], mul=1.0)
 
-        x_rows = const.tile([P, PACK, 2 * FEATURES], BF16)
-        x_view = x[0].rearrange("(c m e) k -> m c (e k)", c=PACK, e=2)
-        for c in range(PACK):
-            nc.sync.dma_start(out=x_rows[:, c, :], in_=x_view[:, c, :])
+        x_rows = const.tile([P, 2, PACK, FEATURES], BF16)
+        x_view = x[0].rearrange("(c m e) k -> e m c k", c=PACK, e=2)
+
+        def load_x(e, c0):
+            nc.sync.dma_start(out=x_rows[:, e, c0 : c0 + 2, :], in_=x_view[e][:, c0 : c0 + 2, :])
+
         wq_codes = const.tile([P, HEADS, FEATURES], U32, align_bytes=64)
         wk_codes = const.tile([P, HEADS, FEATURES], U32, align_bytes=64)
 
@@ -65,10 +66,14 @@ def tile_multiheadattention_pa_e_kernel(tc, x, wq_words, wq_scales, wk_words, wk
                 in_=words[head].rearrange("p n t -> p (n t)").bitcast(I32),
             )
 
+        load_x(0, 0)
+        load_x(0, 2)
         load_scales(wk_planes, wk_scales)
         load_codes(wk_codes, wk_words, 0)
-        load_scales(wq_planes, wq_scales)
         load_codes(wq_codes, wq_words, 0)
+        load_scales(wq_planes, wq_scales)
+        load_x(1, 0)
+        load_x(1, 2)
         for head in range(1, HEADS):
             load_codes(wk_codes, wk_words, head)
             load_codes(wq_codes, wq_words, head)
@@ -77,30 +82,42 @@ def tile_multiheadattention_pa_e_kernel(tc, x, wq_words, wq_scales, wk_words, wk
         x_grouped = const.tile([P, TOKENS * PACK], BF16, align_bytes=64)
         x_codes = const.tile([P, TOKENS], U32, align_bytes=64)
         x_scales = const.tile([P, TOKENS], U8, align_bytes=64)
-        pairs = FEATURES // 2
-        for c in range(PACK):
+
+        def columns(tile_index, tiles=1):
+            return slice(tile_index * P, (tile_index + tiles) * P)
+
+        written = {"scalar": 0, "vector": 0}
+
+        def next_is_scalar():
+            on_scalar = written["scalar"] <= written["vector"]
+            written["scalar" if on_scalar else "vector"] += BANK
+            return on_scalar
+
+        def transpose_x(e, c0, on_scalar):
+            first = PACK * e + c0
             x_bank = psum.tile([P, BANK], F32, tag="bank")
-            for e in range(2):
+            for i in range(2):
                 for u in range(2):
                     nc.tensor.transpose(
-                        x_bank[:, (2 * e + u) * P : (2 * e + u + 1) * P],
-                        x_pairs[:, c, pairs * e + u : pairs * (e + 1) : 2],
+                        x_bank[:, columns(2 * i + u)],
+                        x_pairs[:, e, c0 + i, u::2],
                         identity[:],
                     )
-            nc.scalar.copy(
-                out=x_grouped[:, 2 * P * PACK * c : 2 * P * PACK * (c + 1)]
-                .bitcast(F32)
-                .rearrange("p (e m u) -> p e m u", e=2, u=2),
-                in_=x_bank[:].rearrange("p (e u m) -> p e m u", e=2, u=2),
-            )
-            nc.vector.quantize_mx(
-                out=x_codes[:, 2 * P * c : 2 * P * (c + 1)].bitcast(FP8X4),
-                scales=x_scales[:, 2 * P * c : 2 * P * (c + 1)],
-                in_=x_grouped[:, 2 * P * PACK * c : 2 * P * PACK * (c + 1)],
-            )
+            dst = x_grouped[:, BANK * first : BANK * (first + 2)].bitcast(F32).rearrange("p (a m u) -> p a m u", a=2, u=2)
+            src = x_bank[:].rearrange("p (a u m) -> p a m u", a=2, u=2)
+            if on_scalar:
+                nc.scalar.copy(out=dst, in_=src)
+            else:
+                nc.vector.tensor_copy(out=dst, in_=src)
 
-        def columns(tile_index):
-            return slice(tile_index * P, (tile_index + 1) * P)
+        def quantise_x(e, c0):
+            written["vector"] += 2 * P
+            first = PACK * e + c0
+            nc.vector.quantize_mx(
+                out=x_codes[:, columns(first, 2)].bitcast(FP8X4),
+                scales=x_scales[:, columns(first, 2)],
+                in_=x_grouped[:, BANK * first : BANK * (first + 2)],
+            )
 
         def regroup(bank, on_scalar):
             grouped = stage_pool.tile([P, BANK], BF16, align_bytes=64, tag="grouped")
@@ -118,6 +135,7 @@ def tile_multiheadattention_pa_e_kernel(tc, x, wq_words, wq_scales, wk_words, wk
             return codes, scales
 
         def quantise(grouped, operand, tile_index):
+            written["vector"] += P
             codes, scales = operand
             nc.vector.quantize_mx(
                 out=codes[:, columns(tile_index)].bitcast(FP8X4),
@@ -142,7 +160,7 @@ def tile_multiheadattention_pa_e_kernel(tc, x, wq_words, wq_scales, wk_words, wk
                     start=True,
                     stop=True,
                 )
-            return regroup(q_bank, on_scalar)
+            return regroup(q_bank, on_scalar), queries[head], token_tile
 
         def project_keys(head, j_tile, on_scalar):
             if j_tile == 0:
@@ -152,52 +170,106 @@ def tile_multiheadattention_pa_e_kernel(tc, x, wq_words, wq_scales, wk_words, wk
             for c in range(PACK):
                 nc.tensor.matmul_mx(
                     out=k_bank[:, columns(c)],
-                    lhsT=x_codes[:, columns(2 * c + e)].bitcast(FP8X4),
-                    lhsT_scale=x_scales[:, columns(2 * c + e)],
+                    lhsT=x_codes[:, columns(PACK * e + c)].bitcast(FP8X4),
+                    lhsT_scale=x_scales[:, columns(PACK * e + c)],
                     rhs=wk_codes[:, head, columns(n_tile)].bitcast(FP8X4),
                     rhs_scale=wk_planes[4 * head : P, columns(n_tile)],
                     start=True,
                     stop=True,
                 )
-            return regroup(k_bank, on_scalar)
+            return regroup(k_bank, on_scalar), keys[head], j_tile
 
-        def scores(head, token_tile):
+        rows = {}
+
+        def scores(head, token_tile, half, on_scalar):
             q_codes, q_scales = queries[head]
             k_codes, k_scales = keys[head]
-            rows = out_pool.tile([P, TOKENS], F32, tag="rows")
-            for half in range(2):
-                j_cols = slice(BANK * half, BANK * (half + 1))
-                s_bank = psum.tile([P, BANK], F32, tag="bank")
-                nc.tensor.matmul_mx(
-                    out=s_bank[:],
-                    lhsT=q_codes[:, columns(token_tile)].bitcast(FP8X4),
-                    lhsT_scale=q_scales[:, columns(token_tile)],
-                    rhs=k_codes[:, j_cols].bitcast(FP8X4),
-                    rhs_scale=k_scales[:, j_cols],
-                    start=True,
-                    stop=True,
-                )
-                nc.scalar.mul(out=rows[:, j_cols], in_=s_bank[:], mul=TOKENS**-0.5)
-            c, e = divmod(token_tile, 2)
+            if half == 0:
+                rows[token_tile] = out_pool.tile([P, TOKENS], F32, tag="rows", name="rows")
+            j_cols = slice(BANK * half, BANK * (half + 1))
+            s_bank = psum.tile([P, BANK], F32, tag="bank")
+            nc.tensor.matmul_mx(
+                out=s_bank[:],
+                lhsT=q_codes[:, columns(token_tile)].bitcast(FP8X4),
+                lhsT_scale=q_scales[:, columns(token_tile)],
+                rhs=k_codes[:, j_cols].bitcast(FP8X4),
+                rhs_scale=k_scales[:, j_cols],
+                start=True,
+                stop=True,
+            )
+            dst = rows[token_tile][:, j_cols]
+            if on_scalar:
+                nc.scalar.mul(out=dst, in_=s_bank[:], mul=TOKENS**-0.5)
+            else:
+                nc.vector.tensor_scalar_mul(dst, s_bank[:], TOKENS**-0.5)
+
+        def store(head, token_tile, j_cols):
+            e, c = divmod(token_tile, PACK)
             nc.sync.dma_start(
-                out=out[head, 0].rearrange("(c m e) j -> c e m j", c=PACK, e=2)[c, e],
-                in_=rows[:],
+                out=out[head, 0].rearrange("(c m e) j -> c e m j", c=PACK, e=2)[c, e][:, j_cols],
+                in_=rows[token_tile][:, j_cols],
             )
 
-        for step in range(-K_AHEAD, UNITS):
-            k_unit = step + K_AHEAD
-            q_unit = step + Q_AHEAD
-            project_k = k_unit < UNITS
-            project_q = 0 <= q_unit < UNITS
-            if project_k:
-                k_head, j_tile = divmod(k_unit, TOKEN_TILES)
-                k_grouped = project_keys(k_head, j_tile, j_tile % 4 == 3 or (step < 0 and j_tile % 2 == 1))
-            if project_q:
-                q_head, q_tile = divmod(q_unit, TOKEN_TILES)
-                q_grouped = project_queries(q_head, q_tile, step < 0)
-            if project_k:
-                quantise(k_grouped, keys[k_head], j_tile)
-            if project_q:
-                quantise(q_grouped, queries[q_head], q_tile)
-            if step >= 0:
-                scores(step // TOKEN_TILES, step % TOKEN_TILES)
+        halves = (slice(0, BANK), slice(BANK, TOKENS))
+
+        banks = [(0, a, half) for half in range(2) for a in range(TOKEN_TILES)]
+        banks += [(head, a, half) for head in range(1, HEADS) for a in range(TOKEN_TILES) for half in range(2)]
+        pairs = range(0, TOKEN_TILES, 2)
+        units = [("k", 0, j) for j in range(PACK)] + [("q", 0, a) for a in range(PACK)]
+        for i in range(PACK, TOKEN_TILES, 2):
+            units += [("q", 0, i), ("q", 0, i + 1), ("k", 0, i), ("k", 0, i + 1)]
+        units += [("k", 1, j) for j in range(TOKEN_TILES)] + [("q", 1, 0), ("q", 1, 1)]
+        for head in range(1, HEADS):
+            for a in pairs:
+                if head + 1 < HEADS:
+                    units += [("k", head + 1, a), ("k", head + 1, a + 1)]
+                q_head, q_tile = divmod(TOKEN_TILES * head + a + 2, TOKEN_TILES)
+                if q_head < HEADS:
+                    units += [("q", q_head, q_tile), ("q", q_head, q_tile + 1)]
+        place = {unit: i for i, unit in enumerate(units)}
+
+        def needed(bank):
+            head, a, half = bank
+            reads = [("q", head, a)] + [("k", head, j) for j in range(PACK * half, PACK * (half + 1))]
+            return 1 + max(place[unit] for unit in reads)
+
+        def due(i):
+            return SLACK + max(needed(banks[t]) - (t - i) for t in range(i, len(banks)))
+
+        odd_x = {("q", 0, 1): 0, ("q", 0, 2): 2}
+
+        made = []
+
+        def quantise_made():
+            for unit in made:
+                quantise(*unit)
+            made.clear()
+
+        def make(kind, head, index):
+            if (kind, head, index) in odd_x:
+                c0 = odd_x[(kind, head, index)]
+                transpose_x(1, c0, next_is_scalar())
+                if c0 == 2:
+                    quantise_x(1, 0)
+                    quantise_x(1, 2)
+            project = project_keys if kind == "k" else project_queries
+            unit = project(head, index, next_is_scalar())
+            if len(made) == 2:
+                quantise_made()
+            made.append(unit)
+
+        for c0 in (0, 2):
+            transpose_x(0, c0, True)
+            quantise_x(0, c0)
+        projected = 0
+        for i, (head, a, half) in enumerate(banks):
+            while projected < min(due(i), len(units)):
+                make(*units[projected])
+                projected += 1
+            if projected == len(units):
+                quantise_made()
+            scores(head, a, half, next_is_scalar())
+            if head == 0:
+                store(head, a, halves[half])
+            elif half == 1:
+                store(head, a, slice(0, TOKENS))

@@ -19,7 +19,7 @@ FEATURES = 512
 TOKEN_TILES = TOKENS // P
 UNITS = HEADS * TOKEN_TILES
 
-SLACK = 4
+SLACK = 3
 
 FLOPS = 2 * HEADS * (2 * TOKENS * FEATURES * FEATURES + TOKENS * FEATURES * TOKENS)
 
@@ -90,11 +90,16 @@ def tile_multiheadattention_pa_e_kernel(tc, x, wq_words, wq_scales, wk_words, wk
 
         def next_is_scalar():
             on_scalar = written["scalar"] <= written["vector"]
-            written["scalar" if on_scalar else "vector"] += BANK
+            written["scalar" if on_scalar else "vector"] += 2 * BANK
             return on_scalar
 
-        def transpose_x(e, c0, on_scalar):
-            first = PACK * e + c0
+        def copy_out(dst, src, on_scalar):
+            if on_scalar:
+                nc.scalar.copy(out=dst, in_=src)
+            else:
+                nc.vector.tensor_copy(out=dst, in_=src)
+
+        def transpose_x(e, c0):
             x_bank = psum.tile([P, BANK], F32, tag="bank")
             for i in range(2):
                 for u in range(2):
@@ -103,12 +108,12 @@ def tile_multiheadattention_pa_e_kernel(tc, x, wq_words, wq_scales, wk_words, wk
                         x_pairs[:, e, c0 + i, u::2],
                         identity[:],
                     )
+            return x_bank
+
+        def regroup_x(x_bank, e, c0, on_scalar):
+            first = PACK * e + c0
             dst = x_grouped[:, BANK * first : BANK * (first + 2)].bitcast(F32).rearrange("p (a m u) -> p a m u", a=2, u=2)
-            src = x_bank[:].rearrange("p (a u m) -> p a m u", a=2, u=2)
-            if on_scalar:
-                nc.scalar.copy(out=dst, in_=src)
-            else:
-                nc.vector.tensor_copy(out=dst, in_=src)
+            copy_out(dst, x_bank[:].rearrange("p (a u m) -> p a m u", a=2, u=2), on_scalar)
 
         def quantise_x(e, c0):
             written["vector"] += 2 * P
@@ -119,36 +124,23 @@ def tile_multiheadattention_pa_e_kernel(tc, x, wq_words, wq_scales, wk_words, wk
                 in_=x_grouped[:, BANK * first : BANK * (first + 2)],
             )
 
-        def regroup(bank, on_scalar):
-            grouped = stage_pool.tile([P, BANK], BF16, align_bytes=64, tag="grouped")
-            dst = grouped[:].rearrange("p (w c) -> p w c", c=PACK)
-            src = bank[:].rearrange("p (c w) -> p w c", c=PACK)
-            if on_scalar:
-                nc.scalar.copy(out=dst, in_=src)
-            else:
-                nc.vector.tensor_copy(out=dst, in_=src)
-            return grouped
-
         def new_operand(name):
             codes = operand_pool.tile([P, TOKENS], U32, align_bytes=64, tag=name + "_codes", name=name + "_codes")
             scales = operand_pool.tile([P, TOKENS], U8, align_bytes=64, tag=name + "_scales", name=name + "_scales")
             return codes, scales
 
         def quantise(grouped, operand, tile_index):
-            written["vector"] += P
+            written["vector"] += 2 * P
             codes, scales = operand
             nc.vector.quantize_mx(
-                out=codes[:, columns(tile_index)].bitcast(FP8X4),
-                scales=scales[:, columns(tile_index)],
+                out=codes[:, columns(tile_index, 2)].bitcast(FP8X4),
+                scales=scales[:, columns(tile_index, 2)],
                 in_=grouped[:],
             )
 
-        queries = {}
-        keys = {}
+        operands = {}
 
-        def project_queries(head, token_tile, on_scalar):
-            if token_tile == 0:
-                queries[head] = new_operand("q")
+        def project_queries(head, token_tile):
             q_bank = psum.tile([P, BANK], F32, tag="bank")
             for c in range(PACK):
                 nc.tensor.matmul_mx(
@@ -160,11 +152,9 @@ def tile_multiheadattention_pa_e_kernel(tc, x, wq_words, wq_scales, wk_words, wk
                     start=True,
                     stop=True,
                 )
-            return regroup(q_bank, on_scalar), queries[head], token_tile
+            return q_bank
 
-        def project_keys(head, j_tile, on_scalar):
-            if j_tile == 0:
-                keys[head] = new_operand("k")
+        def project_keys(head, j_tile):
             e, n_tile = divmod(j_tile, PACK)
             k_bank = psum.tile([P, BANK], F32, tag="bank")
             for c in range(PACK):
@@ -177,13 +167,13 @@ def tile_multiheadattention_pa_e_kernel(tc, x, wq_words, wq_scales, wk_words, wk
                     start=True,
                     stop=True,
                 )
-            return regroup(k_bank, on_scalar), keys[head], j_tile
+            return k_bank
 
         rows = {}
 
-        def scores(head, token_tile, half, on_scalar):
-            q_codes, q_scales = queries[head]
-            k_codes, k_scales = keys[head]
+        def multiply(head, token_tile, half):
+            q_codes, q_scales = operands[("q", head)]
+            k_codes, k_scales = operands[("k", head)]
             if half == 0:
                 rows[token_tile] = out_pool.tile([P, TOKENS], F32, tag="rows", name="rows")
             j_cols = slice(BANK * half, BANK * (half + 1))
@@ -197,7 +187,10 @@ def tile_multiheadattention_pa_e_kernel(tc, x, wq_words, wq_scales, wk_words, wk
                 start=True,
                 stop=True,
             )
-            dst = rows[token_tile][:, j_cols]
+            return s_bank
+
+        def scale_out(s_bank, token_tile, half, on_scalar):
+            dst = rows[token_tile][:, BANK * half : BANK * (half + 1)]
             if on_scalar:
                 nc.scalar.mul(out=dst, in_=s_bank[:], mul=TOKENS**-0.5)
             else:
@@ -210,66 +203,69 @@ def tile_multiheadattention_pa_e_kernel(tc, x, wq_words, wq_scales, wk_words, wk
                 in_=rows[token_tile][:, j_cols],
             )
 
-        halves = (slice(0, BANK), slice(BANK, TOKENS))
-
         banks = [(0, a, half) for half in range(2) for a in range(TOKEN_TILES)]
         banks += [(head, a, half) for head in range(1, HEADS) for a in range(TOKEN_TILES) for half in range(2)]
-        pairs = range(0, TOKEN_TILES, 2)
-        units = [("k", 0, j) for j in range(PACK)] + [("q", 0, a) for a in range(PACK)]
-        for i in range(PACK, TOKEN_TILES, 2):
-            units += [("q", 0, i), ("q", 0, i + 1), ("k", 0, i), ("k", 0, i + 1)]
-        units += [("k", 1, j) for j in range(TOKEN_TILES)] + [("q", 1, 0), ("q", 1, 1)]
-        for head in range(1, HEADS):
-            for a in pairs:
-                if head + 1 < HEADS:
-                    units += [("k", head + 1, a), ("k", head + 1, a + 1)]
-                q_head, q_tile = divmod(TOKEN_TILES * head + a + 2, TOKEN_TILES)
-                if q_head < HEADS:
-                    units += [("q", q_head, q_tile), ("q", q_head, q_tile + 1)]
+        units = []
+        for head, a, half in banks:
+            for kind, index in [("k", PACK * half), ("k", PACK * half + 2), ("q", a - a % 2)]:
+                if (kind, head, index) not in units:
+                    units += [(kind, head, index), (kind, head, index + 1)]
         place = {unit: i for i, unit in enumerate(units)}
 
         def needed(bank):
             head, a, half = bank
-            reads = [("q", head, a)] + [("k", head, j) for j in range(PACK * half, PACK * (half + 1))]
-            return 1 + max(place[unit] for unit in reads)
+            return 1 + max(place[("q", head, a)], place[("k", head, PACK * half + PACK - 1)])
 
         def due(i):
             return SLACK + max(needed(banks[t]) - (t - i) for t in range(i, len(banks)))
 
-        odd_x = {("q", 0, 1): 0, ("q", 0, 2): 2}
-
         made = []
 
         def quantise_made():
-            for unit in made:
-                quantise(*unit)
+            for pair in made:
+                quantise(*pair)
             made.clear()
 
-        def make(kind, head, index):
-            if (kind, head, index) in odd_x:
-                c0 = odd_x[(kind, head, index)]
-                transpose_x(1, c0, next_is_scalar())
-                if c0 == 2:
-                    quantise_x(1, 0)
-                    quantise_x(1, 2)
+        def make_pair(kind, head, index):
+            if index == 0:
+                operands[(kind, head)] = new_operand(kind)
             project = project_keys if kind == "k" else project_queries
-            unit = project(head, index, next_is_scalar())
-            if len(made) == 2:
-                quantise_made()
-            made.append(unit)
+            pair = [project(head, index), project(head, index + 1)]
+            grouped = stage_pool.tile([P, 2 * BANK], BF16, align_bytes=64, tag="grouped")
+            on_scalar = next_is_scalar()
+            for i in (1, 0):
+                copy_out(
+                    grouped[:, BANK * i : BANK * (i + 1)].rearrange("p (w c) -> p w c", c=PACK),
+                    pair[i][:].rearrange("p (c w) -> p w c", c=PACK),
+                    on_scalar,
+                )
+            quantise_made()
+            made.append((grouped, operands[(kind, head)], index))
 
         for c0 in (0, 2):
-            transpose_x(0, c0, True)
+            regroup_x(transpose_x(0, c0), 0, c0, True)
             quantise_x(0, c0)
         projected = 0
-        for i, (head, a, half) in enumerate(banks):
-            while projected < min(due(i), len(units)):
-                make(*units[projected])
-                projected += 1
+        for i in range(0, len(banks), 2):
+            while projected < min(due(i + 1), len(units)):
+                if projected == PACK:
+                    pair = [transpose_x(1, 0), transpose_x(1, 2)]
+                    on_scalar = next_is_scalar()
+                    for n in (1, 0):
+                        regroup_x(pair[n], 1, 2 * n, on_scalar)
+                    for n in range(2):
+                        quantise_x(1, 2 * n)
+                make_pair(*units[projected])
+                projected += 2
             if projected == len(units):
                 quantise_made()
-            scores(head, a, half, next_is_scalar())
-            if head == 0:
-                store(head, a, halves[half])
-            elif half == 1:
+            pair = [multiply(*banks[i]), multiply(*banks[i + 1])]
+            on_scalar = next_is_scalar()
+            for n in (1, 0):
+                scale_out(pair[n], *banks[i + n][1:], on_scalar)
+            head, a, half = banks[i]
+            if banks[i + 1][1] == a:
                 store(head, a, slice(0, TOKENS))
+            else:
+                for n in (1, 0):
+                    store(head, banks[i + n][1], slice(BANK * half, BANK * (half + 1)))

@@ -1,3 +1,4 @@
+import math
 from contextlib import ExitStack
 
 import concourse.mybir as mybir
@@ -19,7 +20,12 @@ FEATURES = 512
 TOKEN_TILES = TOKENS // P
 UNITS = HEADS * TOKEN_TILES
 
-SLACK = 3
+PACE = 1.25
+SLACK = 4
+LAST_SLACK = 2
+ALONE = 8
+
+WARM_UP = 5
 
 FLOPS = 2 * HEADS * (2 * TOKENS * FEATURES * FEATURES + TOKENS * FEATURES * TOKENS)
 
@@ -34,15 +40,22 @@ def tile_multiheadattention_pa_e_kernel(tc, x, wq_words, wq_scales, wk_words, wk
         out_pool = ctx.enter_context(tc.tile_pool(name="scores", bufs=UNITS))
         psum = ctx.enter_context(tc.psum_pool(name="psum", bufs=8))
 
-        identity = const.tile([P, P], F32)
-        make_identity(nc, identity[:])
         wq_planes = const.tile([P, FEATURES], U8, align_bytes=64)
         wk_planes = const.tile([P, FEATURES], U8, align_bytes=64)
-        nc.vector.memset(wk_planes[:].bitcast(I32), 0)
         nc.vector.memset(wq_planes[:].bitcast(I32), 0)
+        nc.vector.memset(wk_planes[:].bitcast(I32), 0)
         warm = const.tile([P, 1], F32)
         nc.vector.memset(warm[:], 0.0)
         nc.scalar.mul(out=warm[:], in_=warm[:], mul=1.0)
+
+        zeros = const.tile([P, BANK], BF16)
+        nc.gpsimd.memset(zeros[:].bitcast(I32), 0)
+        warm_bank = psum.tile([P, BANK], F32, tag="bank")
+        for i in range(WARM_UP):
+            nc.tensor.matmul(warm_bank[:], lhsT=zeros[:, 0:P], rhs=zeros[:], start=True, stop=True)
+
+        identity = const.tile([P, P], F32)
+        make_identity(nc, identity[:])
 
         x_rows = const.tile([P, 2, PACK, FEATURES], BF16)
         x_view = x[0].rearrange("(c m e) k -> e m c k", c=PACK, e=2)
@@ -68,10 +81,10 @@ def tile_multiheadattention_pa_e_kernel(tc, x, wq_words, wq_scales, wk_words, wk
 
         load_x(0, 0)
         load_x(0, 2)
-        load_scales(wk_planes, wk_scales)
-        load_codes(wk_codes, wk_words, 0)
-        load_codes(wq_codes, wq_words, 0)
         load_scales(wq_planes, wq_scales)
+        load_codes(wq_codes, wq_words, 0)
+        load_codes(wk_codes, wk_words, 0)
+        load_scales(wk_planes, wk_scales)
         load_x(1, 0)
         load_x(1, 2)
         for head in range(1, HEADS):
@@ -88,10 +101,19 @@ def tile_multiheadattention_pa_e_kernel(tc, x, wq_words, wq_scales, wk_words, wk
 
         written = {"scalar": 0, "vector": 0}
 
-        def next_is_scalar():
+        def next_is_scalar(count):
             on_scalar = written["scalar"] <= written["vector"]
-            written["scalar" if on_scalar else "vector"] += 2 * BANK
+            written["scalar" if on_scalar else "vector"] += count * BANK
             return on_scalar
+
+        def empty(copies, alone):
+            if alone:
+                for copy in copies:
+                    copy(next_is_scalar(1))
+            else:
+                on_scalar = next_is_scalar(2)
+                copies[1](on_scalar)
+                copies[0](on_scalar)
 
         def copy_out(dst, src, on_scalar):
             if on_scalar:
@@ -203,9 +225,11 @@ def tile_multiheadattention_pa_e_kernel(tc, x, wq_words, wq_scales, wk_words, wk
                 in_=rows[token_tile][:, j_cols],
             )
 
+        last = HEADS - 1
         banks = [(0, a, half) for half in range(2) for a in range(TOKEN_TILES)]
-        banks += [(head, a, half) for head in range(1, HEADS) for a in range(TOKEN_TILES) for half in range(2)]
-        units = []
+        banks += [(head, a, half) for head in range(1, last) for a in range(TOKEN_TILES) for half in range(2)]
+        banks += [(last, a, half) for half in range(2) for a in range(TOKEN_TILES)]
+        units = [("q", 0, 0), ("q", 0, 1)]
         for head, a, half in banks:
             for kind, index in [("k", PACK * half), ("k", PACK * half + 2), ("q", a - a % 2)]:
                 if (kind, head, index) not in units:
@@ -217,7 +241,8 @@ def tile_multiheadattention_pa_e_kernel(tc, x, wq_words, wq_scales, wk_words, wk
             return 1 + max(place[("q", head, a)], place[("k", head, PACK * half + PACK - 1)])
 
         def due(i):
-            return SLACK + max(needed(banks[t]) - (t - i) for t in range(i, len(banks)))
+            slack = LAST_SLACK if needed(banks[i]) > len(units) - 2 * TOKEN_TILES else SLACK
+            return slack + math.ceil(max(needed(banks[t]) - PACE * (t - i) for t in range(i, len(banks))))
 
         made = []
 
@@ -232,13 +257,12 @@ def tile_multiheadattention_pa_e_kernel(tc, x, wq_words, wq_scales, wk_words, wk
             project = project_keys if kind == "k" else project_queries
             pair = [project(head, index), project(head, index + 1)]
             grouped = stage_pool.tile([P, 2 * BANK], BF16, align_bytes=64, tag="grouped")
-            on_scalar = next_is_scalar()
-            for i in (1, 0):
-                copy_out(
-                    grouped[:, BANK * i : BANK * (i + 1)].rearrange("p (w c) -> p w c", c=PACK),
-                    pair[i][:].rearrange("p (c w) -> p w c", c=PACK),
-                    on_scalar,
-                )
+
+            def regroup(i):
+                dst = grouped[:, BANK * i : BANK * (i + 1)].rearrange("p (w c) -> p w c", c=PACK)
+                return lambda on_scalar: copy_out(dst, pair[i][:].rearrange("p (c w) -> p w c", c=PACK), on_scalar)
+
+            empty([regroup(0), regroup(1)], place[(kind, head, index)] < ALONE)
             quantise_made()
             made.append((grouped, operands[(kind, head)], index))
 
@@ -249,10 +273,8 @@ def tile_multiheadattention_pa_e_kernel(tc, x, wq_words, wq_scales, wk_words, wk
         for i in range(0, len(banks), 2):
             while projected < min(due(i + 1), len(units)):
                 if projected == PACK:
-                    pair = [transpose_x(1, 0), transpose_x(1, 2)]
-                    on_scalar = next_is_scalar()
-                    for n in (1, 0):
-                        regroup_x(pair[n], 1, 2 * n, on_scalar)
+                    odd = [transpose_x(1, 0), transpose_x(1, 2)]
+                    empty([lambda on_scalar, n=n: regroup_x(odd[n], 1, 2 * n, on_scalar) for n in range(2)], False)
                     for n in range(2):
                         quantise_x(1, 2 * n)
                 make_pair(*units[projected])
@@ -260,12 +282,13 @@ def tile_multiheadattention_pa_e_kernel(tc, x, wq_words, wq_scales, wk_words, wk
             if projected == len(units):
                 quantise_made()
             pair = [multiply(*banks[i]), multiply(*banks[i + 1])]
-            on_scalar = next_is_scalar()
-            for n in (1, 0):
-                scale_out(pair[n], *banks[i + n][1:], on_scalar)
             head, a, half = banks[i]
+            empty(
+                [lambda on_scalar, n=n: scale_out(pair[n], *banks[i + n][1:], on_scalar) for n in range(2)],
+                head == last,
+            )
             if banks[i + 1][1] == a:
                 store(head, a, slice(0, TOKENS))
             else:
-                for n in (1, 0):
+                for n in range(2):
                     store(head, banks[i + n][1], slice(BANK * half, BANK * (half + 1)))

@@ -1,4 +1,3 @@
-import math
 from contextlib import ExitStack
 
 import concourse.mybir as mybir
@@ -20,10 +19,8 @@ FEATURES = 512
 TOKEN_TILES = TOKENS // P
 UNITS = HEADS * TOKEN_TILES
 
-PACE = 1.25
-SLACK = 4
-LAST_SLACK = 2
-ALONE = 8
+SLACK = 3
+ALONE = 6
 
 WARM_UP = 5
 
@@ -121,9 +118,9 @@ def tile_multiheadattention_pa_e_kernel(tc, x, wq_words, wq_scales, wk_words, wk
             else:
                 nc.vector.tensor_copy(out=dst, in_=src)
 
-        def transpose_x(e, c0):
+        def transpose_x(e, c0, tiles):
             x_bank = psum.tile([P, BANK], F32, tag="bank")
-            for i in range(2):
+            for i in range(tiles):
                 for u in range(2):
                     nc.tensor.transpose(
                         x_bank[:, columns(2 * i + u)],
@@ -132,18 +129,22 @@ def tile_multiheadattention_pa_e_kernel(tc, x, wq_words, wq_scales, wk_words, wk
                     )
             return x_bank
 
-        def regroup_x(x_bank, e, c0, on_scalar):
+        def regroup_x(x_bank, e, c0, tiles, on_scalar):
             first = PACK * e + c0
-            dst = x_grouped[:, BANK * first : BANK * (first + 2)].bitcast(F32).rearrange("p (a m u) -> p a m u", a=2, u=2)
-            copy_out(dst, x_bank[:].rearrange("p (a u m) -> p a m u", a=2, u=2), on_scalar)
+            dst = x_grouped[:, BANK * first : BANK * (first + tiles)].bitcast(F32)
+            copy_out(
+                dst.rearrange("p (a m u) -> p a m u", a=tiles, u=2),
+                x_bank[:, columns(0, 2 * tiles)].rearrange("p (a u m) -> p a m u", a=tiles, u=2),
+                on_scalar,
+            )
 
-        def quantise_x(e, c0):
-            written["vector"] += 2 * P
+        def quantise_x(e, c0, tiles):
+            written["vector"] += tiles * P
             first = PACK * e + c0
             nc.vector.quantize_mx(
-                out=x_codes[:, columns(first, 2)].bitcast(FP8X4),
-                scales=x_scales[:, columns(first, 2)],
-                in_=x_grouped[:, BANK * first : BANK * (first + 2)],
+                out=x_codes[:, columns(first, tiles)].bitcast(FP8X4),
+                scales=x_scales[:, columns(first, tiles)],
+                in_=x_grouped[:, BANK * first : BANK * (first + tiles)],
             )
 
         def new_operand(name):
@@ -228,7 +229,8 @@ def tile_multiheadattention_pa_e_kernel(tc, x, wq_words, wq_scales, wk_words, wk
         last = HEADS - 1
         banks = [(0, a, half) for half in range(2) for a in range(TOKEN_TILES)]
         banks += [(head, a, half) for head in range(1, last) for a in range(TOKEN_TILES) for half in range(2)]
-        banks += [(last, a, half) for half in range(2) for a in range(TOKEN_TILES)]
+        banks += [(last, a, half) for half in range(2) for a in range(PACK)]
+        banks += [(last, a, half) for a in range(PACK, TOKEN_TILES) for half in range(2)]
         units = [("q", 0, 0), ("q", 0, 1)]
         for head, a, half in banks:
             for kind, index in [("k", PACK * half), ("k", PACK * half + 2), ("q", a - a % 2)]:
@@ -241,8 +243,7 @@ def tile_multiheadattention_pa_e_kernel(tc, x, wq_words, wq_scales, wk_words, wk
             return 1 + max(place[("q", head, a)], place[("k", head, PACK * half + PACK - 1)])
 
         def due(i):
-            slack = LAST_SLACK if needed(banks[i]) > len(units) - 2 * TOKEN_TILES else SLACK
-            return slack + math.ceil(max(needed(banks[t]) - PACE * (t - i) for t in range(i, len(banks))))
+            return SLACK + max(needed(banks[t]) - (t - i) for t in range(i, len(banks)))
 
         made = []
 
@@ -266,17 +267,18 @@ def tile_multiheadattention_pa_e_kernel(tc, x, wq_words, wq_scales, wk_words, wk
             quantise_made()
             made.append((grouped, operands[(kind, head)], index))
 
-        for c0 in (0, 2):
-            regroup_x(transpose_x(0, c0), 0, c0, True)
-            quantise_x(0, c0)
+        for c in range(PACK):
+            written["scalar"] += 2 * P
+            regroup_x(transpose_x(0, c, 1), 0, c, 1, True)
+            quantise_x(0, c, 1)
         projected = 0
         for i in range(0, len(banks), 2):
             while projected < min(due(i + 1), len(units)):
                 if projected == PACK:
-                    odd = [transpose_x(1, 0), transpose_x(1, 2)]
-                    empty([lambda on_scalar, n=n: regroup_x(odd[n], 1, 2 * n, on_scalar) for n in range(2)], False)
+                    odd = [transpose_x(1, 0, 2), transpose_x(1, 2, 2)]
+                    empty([lambda on_scalar, n=n: regroup_x(odd[n], 1, 2 * n, 2, on_scalar) for n in range(2)], False)
                     for n in range(2):
-                        quantise_x(1, 2 * n)
+                        quantise_x(1, 2 * n, 2)
                 make_pair(*units[projected])
                 projected += 2
             if projected == len(units):
@@ -285,7 +287,7 @@ def tile_multiheadattention_pa_e_kernel(tc, x, wq_words, wq_scales, wk_words, wk
             head, a, half = banks[i]
             empty(
                 [lambda on_scalar, n=n: scale_out(pair[n], *banks[i + n][1:], on_scalar) for n in range(2)],
-                head == last,
+                head >= HEADS // 2,
             )
             if banks[i + 1][1] == a:
                 store(head, a, slice(0, TOKENS))

@@ -22,7 +22,8 @@ UNITS = HEADS * TOKEN_TILES
 SLACK = 3
 ALONE = 6
 
-WARM_UP = 5
+WARM_UP = 6
+KEEP_WARM = 2
 
 FLOPS = 2 * HEADS * (2 * TOKENS * FEATURES * FEATURES + TOKENS * FEATURES * TOKENS)
 
@@ -37,6 +38,8 @@ def tile_multiheadattention_pa_e_kernel(tc, x, wq_words, wq_scales, wk_words, wk
         out_pool = ctx.enter_context(tc.tile_pool(name="scores", bufs=UNITS))
         psum = ctx.enter_context(tc.psum_pool(name="psum", bufs=8))
 
+        zeros = const.tile([P, BANK], BF16)
+        nc.vector.memset(zeros[:].bitcast(I32), 0)
         wq_planes = const.tile([P, FEATURES], U8, align_bytes=64)
         wk_planes = const.tile([P, FEATURES], U8, align_bytes=64)
         nc.vector.memset(wq_planes[:].bitcast(I32), 0)
@@ -45,12 +48,13 @@ def tile_multiheadattention_pa_e_kernel(tc, x, wq_words, wq_scales, wk_words, wk
         nc.vector.memset(warm[:], 0.0)
         nc.scalar.mul(out=warm[:], in_=warm[:], mul=1.0)
 
-        zeros = const.tile([P, BANK], BF16)
-        nc.gpsimd.memset(zeros[:].bitcast(I32), 0)
-        warm_bank = psum.tile([P, BANK], F32, tag="bank")
-        for i in range(WARM_UP):
-            nc.tensor.matmul(warm_bank[:], lhsT=zeros[:, 0:P], rhs=zeros[:], start=True, stop=True)
 
+        def keep_warm(count):
+            warm_bank = psum.tile([P, BANK], F32, tag="bank", name="warm_bank")
+            for i in range(count):
+                nc.tensor.matmul(warm_bank[:], lhsT=zeros[:, 0:P], rhs=zeros[:], start=True, stop=True)
+
+        keep_warm(WARM_UP)
         identity = const.tile([P, P], F32)
         make_identity(nc, identity[:])
 
@@ -271,6 +275,7 @@ def tile_multiheadattention_pa_e_kernel(tc, x, wq_words, wq_scales, wk_words, wk
             written["scalar"] += 2 * P
             regroup_x(transpose_x(0, c, 1), 0, c, 1, True)
             quantise_x(0, c, 1)
+        keep_warm(KEEP_WARM)
         projected = 0
         for i in range(0, len(banks), 2):
             while projected < min(due(i + 1), len(units)):

@@ -22,7 +22,7 @@ UNITS = HEADS * TOKEN_TILES
 SLACK = 3
 ALONE = 6
 
-WARM_UP = 6
+WARM_UP = 5
 KEEP_WARM = 2
 
 FLOPS = 2 * HEADS * (2 * TOKENS * FEATURES * FEATURES + TOKENS * FEATURES * TOKENS)
@@ -122,34 +122,31 @@ def tile_multiheadattention_pa_e_kernel(tc, x, wq_words, wq_scales, wk_words, wk
             else:
                 nc.vector.tensor_copy(out=dst, in_=src)
 
-        def transpose_x(e, c0, tiles):
+        def transpose_x(e, c):
             x_bank = psum.tile([P, BANK], F32, tag="bank")
-            for i in range(tiles):
-                for u in range(2):
-                    nc.tensor.transpose(
-                        x_bank[:, columns(2 * i + u)],
-                        x_pairs[:, e, c0 + i, u::2],
-                        identity[:],
-                    )
-            return x_bank
+            for u in range(2):
+                nc.tensor.transpose(x_bank[:, columns(u)], x_pairs[:, e, c, u::2], identity[:])
+            a = PACK * e + c
+            dst = x_grouped[:, BANK * a : BANK * (a + 1)].bitcast(F32).rearrange("p (m u) -> p m u", u=2)
+            on_scalar = c % 2 == 0
+            written["scalar" if on_scalar else "vector"] += 2 * P
+            copy_out(dst, x_bank[:, columns(0, 2)].rearrange("p (u m) -> p m u", u=2), on_scalar)
 
-        def regroup_x(x_bank, e, c0, tiles, on_scalar):
-            first = PACK * e + c0
-            dst = x_grouped[:, BANK * first : BANK * (first + tiles)].bitcast(F32)
-            copy_out(
-                dst.rearrange("p (a m u) -> p a m u", a=tiles, u=2),
-                x_bank[:, columns(0, 2 * tiles)].rearrange("p (a u m) -> p a m u", a=tiles, u=2),
-                on_scalar,
-            )
-
-        def quantise_x(e, c0, tiles):
-            written["vector"] += tiles * P
-            first = PACK * e + c0
+        def quantise_x(e, c):
+            written["vector"] += P
+            a = PACK * e + c
             nc.vector.quantize_mx(
-                out=x_codes[:, columns(first, tiles)].bitcast(FP8X4),
-                scales=x_scales[:, columns(first, tiles)],
-                in_=x_grouped[:, BANK * first : BANK * (first + tiles)],
+                out=x_codes[:, columns(a)].bitcast(FP8X4),
+                scales=x_scales[:, columns(a)],
+                in_=x_grouped[:, BANK * a : BANK * (a + 1)],
             )
+
+        def take_x(e):
+            for c in range(PACK):
+                transpose_x(e, c)
+                if c > 0:
+                    quantise_x(e, c - 1)
+            quantise_x(e, PACK - 1)
 
         def new_operand(name):
             codes = operand_pool.tile([P, TOKENS], U32, align_bytes=64, tag=name + "_codes", name=name + "_codes")
@@ -271,19 +268,13 @@ def tile_multiheadattention_pa_e_kernel(tc, x, wq_words, wq_scales, wk_words, wk
             quantise_made()
             made.append((grouped, operands[(kind, head)], index))
 
-        for c in range(PACK):
-            written["scalar"] += 2 * P
-            regroup_x(transpose_x(0, c, 1), 0, c, 1, True)
-            quantise_x(0, c, 1)
+        take_x(0)
         keep_warm(KEEP_WARM)
         projected = 0
         for i in range(0, len(banks), 2):
             while projected < min(due(i + 1), len(units)):
                 if projected == PACK:
-                    odd = [transpose_x(1, 0, 2), transpose_x(1, 2, 2)]
-                    empty([lambda on_scalar, n=n: regroup_x(odd[n], 1, 2 * n, 2, on_scalar) for n in range(2)], False)
-                    for n in range(2):
-                        quantise_x(1, 2 * n, 2)
+                    take_x(1)
                 make_pair(*units[projected])
                 projected += 2
             if projected == len(units):
@@ -292,7 +283,7 @@ def tile_multiheadattention_pa_e_kernel(tc, x, wq_words, wq_scales, wk_words, wk
             head, a, half = banks[i]
             empty(
                 [lambda on_scalar, n=n: scale_out(pair[n], *banks[i + n][1:], on_scalar) for n in range(2)],
-                head >= HEADS // 2,
+                head == last,
             )
             if banks[i + 1][1] == a:
                 store(head, a, slice(0, TOKENS))

@@ -133,7 +133,7 @@ def tile_multiheadattention_pa_e_kernel(tc, x, wq_words, wq_scales, wk_words, wk
             copy_out(dst, x_bank[:, columns(0, 2)].rearrange("p (u m) -> p m u", u=2), on_scalar)
 
         def quantise_x(e, c):
-            written["vector"] += P
+            written["vector"] += 9 * P // 8
             a = PACK * e + c
             nc.vector.quantize_mx(
                 out=x_codes[:, columns(a)].bitcast(FP8X4),
@@ -154,7 +154,7 @@ def tile_multiheadattention_pa_e_kernel(tc, x, wq_words, wq_scales, wk_words, wk
             return codes, scales
 
         def quantise(grouped, operand, tile_index):
-            written["vector"] += 2 * P
+            written["vector"] += 9 * P // 4
             codes, scales = operand
             nc.vector.quantize_mx(
                 out=codes[:, columns(tile_index, 2)].bitcast(FP8X4),

from contextlib import ExitStack

import concourse.mybir as mybir
from concourse.masks import make_identity

F32 = mybir.dt.float32
BF16 = mybir.dt.bfloat16
I32 = mybir.dt.int32
U32 = mybir.dt.uint32
U8 = mybir.dt.uint8
FP8X4 = mybir.dt.float8_e4m3fn_x4

P = 128
PACK = 4
BANK = 512
HEADS = 4
TOKENS = 1024
FEATURES = 512
TOKEN_TILES = TOKENS // P
UNITS = HEADS * TOKEN_TILES

SLACK = 3
ALONE = 6

WARM_UP = 5
KEEP_WARM = 2

FLOPS = 2 * HEADS * (2 * TOKENS * FEATURES * FEATURES + TOKENS * FEATURES * TOKENS)


def tile_multiheadattention_pa_e_kernel(tc, x, wq_words, wq_scales, wk_words, wk_scales, out):
    nc = tc.nc
    with ExitStack() as ctx:
        ctx.enter_context(tc.manual_schedule())
        const = ctx.enter_context(tc.tile_pool(name="const", bufs=1))
        stage_pool = ctx.enter_context(tc.tile_pool(name="stage", bufs=8))
        operand_pool = ctx.enter_context(tc.tile_pool(name="operands", bufs=2))
        out_pool = ctx.enter_context(tc.tile_pool(name="scores", bufs=UNITS))
        psum = ctx.enter_context(tc.psum_pool(name="psum", bufs=8))

        zeros = const.tile([P, BANK], BF16)
        nc.vector.memset(zeros[:].bitcast(I32), 0)
        wq_planes = const.tile([P, FEATURES], U8, align_bytes=64)
        wk_planes = const.tile([P, FEATURES], U8, align_bytes=64)
        nc.vector.memset(wq_planes[:].bitcast(I32), 0)
        nc.vector.memset(wk_planes[:].bitcast(I32), 0)
        warm = const.tile([P, 1], F32)
        nc.vector.memset(warm[:], 0.0)
        nc.scalar.mul(out=warm[:], in_=warm[:], mul=1.0)


        def keep_warm(count):
            warm_bank = psum.tile([P, BANK], F32, tag="bank", name="warm_bank")
            for i in range(count):
                nc.tensor.matmul(warm_bank[:], lhsT=zeros[:, 0:P], rhs=zeros[:], start=True, stop=True)

        keep_warm(WARM_UP)
        identity = const.tile([P, P], F32)
        make_identity(nc, identity[:])

        x_rows = const.tile([P, 2, PACK, FEATURES], BF16)
        x_view = x[0].rearrange("(c m e) k -> e m c k", c=PACK, e=2)

        def load_x(e, c0):
            nc.sync.dma_start(out=x_rows[:, e, c0 : c0 + 2, :], in_=x_view[e][:, c0 : c0 + 2, :])

        wq_codes = const.tile([P, HEADS, FEATURES], U32, align_bytes=64)
        wk_codes = const.tile([P, HEADS, FEATURES], U32, align_bytes=64)

        def load_scales(planes, scales):
            for quadrant in range(4):
                nc.sync.dma_start(
                    out=planes[32 * quadrant : 32 * quadrant + 4 * HEADS, :].bitcast(I32),
                    in_=scales[:, 4 * quadrant : 4 * quadrant + 4, :].bitcast(I32),
                )

        def load_codes(codes, words, head):
            nc.sync.dma_start(
                out=codes[:, head, :].bitcast(I32),
                in_=words[head].rearrange("p n t -> p (n t)").bitcast(I32),
            )

        load_x(0, 0)
        load_x(0, 2)
        load_scales(wq_planes, wq_scales)
        load_codes(wq_codes, wq_words, 0)
        load_codes(wk_codes, wk_words, 0)
        load_scales(wk_planes, wk_scales)
        load_x(1, 0)
        load_x(1, 2)
        for head in range(1, HEADS):
            load_codes(wk_codes, wk_words, head)
            load_codes(wq_codes, wq_words, head)

        x_pairs = x_rows[:].bitcast(F32)
        x_grouped = const.tile([P, TOKENS * PACK], BF16, align_bytes=64)
        x_codes = const.tile([P, TOKENS], U32, align_bytes=64)
        x_scales = const.tile([P, TOKENS], U8, align_bytes=64)

        def columns(tile_index, tiles=1):
            return slice(tile_index * P, (tile_index + tiles) * P)

        written = {"scalar": 0, "vector": 0}

        def next_is_scalar(count):
            on_scalar = written["scalar"] <= written["vector"]
            written["scalar" if on_scalar else "vector"] += count * BANK
            return on_scalar

        def empty(copies, alone):
            if alone:
                for copy in copies:
                    copy(next_is_scalar(1))
            else:
                on_scalar = next_is_scalar(2)
                copies[1](on_scalar)
                copies[0](on_scalar)

        def copy_out(dst, src, on_scalar):
            if on_scalar:
                nc.scalar.copy(out=dst, in_=src)
            else:
                nc.vector.tensor_copy(out=dst, in_=src)

        def transpose_x(e, c):
            x_bank = psum.tile([P, BANK], F32, tag="bank")
            for u in range(2):
                nc.tensor.transpose(x_bank[:, columns(u)], x_pairs[:, e, c, u::2], identity[:])
            a = PACK * e + c
            dst = x_grouped[:, BANK * a : BANK * (a + 1)].bitcast(F32).rearrange("p (m u) -> p m u", u=2)
            on_scalar = c % 2 == 0
            written["scalar" if on_scalar else "vector"] += 2 * P
            copy_out(dst, x_bank[:, columns(0, 2)].rearrange("p (u m) -> p m u", u=2), on_scalar)

        def quantise_x(e, c):
            written["vector"] += 9 * P // 8
            a = PACK * e + c
            nc.vector.quantize_mx(
                out=x_codes[:, columns(a)].bitcast(FP8X4),
                scales=x_scales[:, columns(a)],
                in_=x_grouped[:, BANK * a : BANK * (a + 1)],
            )

        def take_x(e):
            for c in range(PACK):
                transpose_x(e, c)
                if c > 0:
                    quantise_x(e, c - 1)
            quantise_x(e, PACK - 1)

        def new_operand(name):
            codes = operand_pool.tile([P, TOKENS], U32, align_bytes=64, tag=name + "_codes", name=name + "_codes")
            scales = operand_pool.tile([P, TOKENS], U8, align_bytes=64, tag=name + "_scales", name=name + "_scales")
            return codes, scales

        def quantise(grouped, operand, tile_index):
            written["vector"] += 9 * P // 4
            codes, scales = operand
            nc.vector.quantize_mx(
                out=codes[:, columns(tile_index, 2)].bitcast(FP8X4),
                scales=scales[:, columns(tile_index, 2)],
                in_=grouped[:],
            )

        operands = {}

        def project_queries(head, token_tile):
            q_bank = psum.tile([P, BANK], F32, tag="bank")
            for c in range(PACK):
                nc.tensor.matmul_mx(
                    out=q_bank[:, columns(c)],
                    lhsT=wq_codes[:, head, columns(c)].bitcast(FP8X4),
                    lhsT_scale=wq_planes[4 * head : P, columns(c)],
                    rhs=x_codes[:, columns(token_tile)].bitcast(FP8X4),
                    rhs_scale=x_scales[:, columns(token_tile)],
                    start=True,
                    stop=True,
                )
            return q_bank

        def project_keys(head, j_tile):
            e, n_tile = divmod(j_tile, PACK)
            k_bank = psum.tile([P, BANK], F32, tag="bank")
            for c in range(PACK):
                nc.tensor.matmul_mx(
                    out=k_bank[:, columns(c)],
                    lhsT=x_codes[:, columns(PACK * e + c)].bitcast(FP8X4),
                    lhsT_scale=x_scales[:, columns(PACK * e + c)],
                    rhs=wk_codes[:, head, columns(n_tile)].bitcast(FP8X4),
                    rhs_scale=wk_planes[4 * head : P, columns(n_tile)],
                    start=True,
                    stop=True,
                )
            return k_bank

        rows = {}

        def multiply(head, token_tile, half):
            q_codes, q_scales = operands[("q", head)]
            k_codes, k_scales = operands[("k", head)]
            if half == 0:
                rows[token_tile] = out_pool.tile([P, TOKENS], F32, tag="rows", name="rows")
            j_cols = slice(BANK * half, BANK * (half + 1))
            s_bank = psum.tile([P, BANK], F32, tag="bank")
            nc.tensor.matmul_mx(
                out=s_bank[:],
                lhsT=q_codes[:, columns(token_tile)].bitcast(FP8X4),
                lhsT_scale=q_scales[:, columns(token_tile)],
                rhs=k_codes[:, j_cols].bitcast(FP8X4),
                rhs_scale=k_scales[:, j_cols],
                start=True,
                stop=True,
            )
            return s_bank

        def scale_out(s_bank, token_tile, half, on_scalar):
            dst = rows[token_tile][:, BANK * half : BANK * (half + 1)]
            if on_scalar:
                nc.scalar.mul(out=dst, in_=s_bank[:], mul=TOKENS**-0.5)
            else:
                nc.vector.tensor_scalar_mul(dst, s_bank[:], TOKENS**-0.5)

        def store(head, token_tile, j_cols):
            e, c = divmod(token_tile, PACK)
            nc.sync.dma_start(
                out=out[head, 0].rearrange("(c m e) j -> c e m j", c=PACK, e=2)[c, e][:, j_cols],
                in_=rows[token_tile][:, j_cols],
            )

        last = HEADS - 1
        banks = [(0, a, half) for half in range(2) for a in range(TOKEN_TILES)]
        banks += [(head, a, half) for head in range(1, last) for a in range(TOKEN_TILES) for half in range(2)]
        banks += [(last, a, half) for half in range(2) for a in range(PACK)]
        banks += [(last, a, half) for a in range(PACK, TOKEN_TILES) for half in range(2)]
        units = [("q", 0, 0), ("q", 0, 1)]
        for head, a, half in banks:
            for kind, index in [("k", PACK * half), ("k", PACK * half + 2), ("q", a - a % 2)]:
                if (kind, head, index) not in units:
                    units += [(kind, head, index), (kind, head, index + 1)]
        place = {unit: i for i, unit in enumerate(units)}

        def needed(bank):
            head, a, half = bank
            return 1 + max(place[("q", head, a)], place[("k", head, PACK * half + PACK - 1)])

        def due(i):
            return SLACK + max(needed(banks[t]) - (t - i) for t in range(i, len(banks)))

        made = []

        def quantise_made():
            for pair in made:
                quantise(*pair)
            made.clear()

        def make_pair(kind, head, index):
            if index == 0:
                operands[(kind, head)] = new_operand(kind)
            project = project_keys if kind == "k" else project_queries
            pair = [project(head, index), project(head, index + 1)]
            grouped = stage_pool.tile([P, 2 * BANK], BF16, align_bytes=64, tag="grouped")

            def regroup(i):
                dst = grouped[:, BANK * i : BANK * (i + 1)].rearrange("p (w c) -> p w c", c=PACK)
                return lambda on_scalar: copy_out(dst, pair[i][:].rearrange("p (c w) -> p w c", c=PACK), on_scalar)

            empty([regroup(0), regroup(1)], place[(kind, head, index)] < ALONE)
            quantise_made()
            made.append((grouped, operands[(kind, head)], index))

        take_x(0)
        keep_warm(KEEP_WARM)
        projected = 0
        for i in range(0, len(banks), 2):
            while projected < min(due(i + 1), len(units)):
                if projected == PACK:
                    take_x(1)
                make_pair(*units[projected])
                projected += 2
            if projected == len(units):
                quantise_made()
            pair = [multiply(*banks[i]), multiply(*banks[i + 1])]
            head, a, half = banks[i]
            empty(
                [lambda on_scalar, n=n: scale_out(pair[n], *banks[i + n][1:], on_scalar) for n in range(2)],
                head == last,
            )
            if banks[i + 1][1] == a:
                store(head, a, slice(0, TOKENS))
            else:
                for n in range(2):
                    store(head, banks[i + n][1], slice(BANK * half, BANK * (half + 1)))
